import numpy as np
import ml_dtypes


def mxq(x, axis, fmt="e4m3"):
    dtype, down = {"e4m3": (ml_dtypes.float8_e4m3fn, 7), "e5m2": (ml_dtypes.float8_e5m2, 14)}[fmt]
    v = np.moveaxis(np.asarray(x, np.float32).astype(ml_dtypes.bfloat16).astype(np.float64), axis, -1)
    blocks = v.reshape(v.shape[:-1] + (-1, 32))
    amax = np.abs(blocks).max(-1, keepdims=True)
    byte = np.maximum(np.where(amax > 0, np.frexp(amax)[1] - 1 + 127, 0) - down, 1)
    scale = np.exp2(byte - 127.0)
    codes = (blocks / scale).astype(np.float32).astype(dtype).astype(np.float64)
    return np.moveaxis((codes * scale).reshape(v.shape), -1, axis)


WIDE = False


def mx_kscale(k):
    if not WIDE:
        return np.ones(k)
    levels = np.array([10, -10, 5, -5, 0])
    a = np.random.permutation(np.resize(levels, k // 512 * 4)).reshape(k // 512, 4)
    idx = np.arange(k)
    return np.exp2(a[idx // 512, idx % 128 // 32])


BF16 = ml_dtypes.bfloat16


def bf(x):
    return np.asarray(x, np.float32).astype(BF16)


def f64(x):
    return np.asarray(x).astype(np.float64)


E2M1 = np.array([0.0, 0.5, 1.0, 1.5, 2.0, 3.0, 4.0, 6.0, -0.0, -0.5, -1.0, -1.5, -2.0, -3.0, -4.0, -6.0])


def pack_weight(w, fmt):
    k, n = w.shape
    w = f64(bf(w)).reshape(k // 32, 32, n)
    amax = np.abs(w).max(1)
    if fmt == "e4m3":
        byte = np.frexp(amax)[1] - 1 + 127 - 7
    else:
        mant, ex = np.frexp(amax / 6.0)
        byte = np.where(mant > 0.5, ex, ex - 1) + 127
    byte = np.clip(np.where(amax > 0, byte, 1), 1, 254)
    scaled = (w * np.exp2(127.0 - byte)[:, None, :]).reshape(k, n).astype(np.float32)
    by_word = np.ascontiguousarray(scaled.reshape(k // 512, 128, 4, n).transpose(0, 1, 3, 2))
    if fmt == "e4m3":
        words = by_word.astype(ml_dtypes.float8_e4m3fn).view(np.uint8)
    else:
        c = by_word.astype(ml_dtypes.float4_e2m1fn).view(np.uint8) & 0xF
        words = c[..., 0::2] | (c[..., 1::2] << 4)
    return np.ascontiguousarray(words), np.ascontiguousarray(byte.astype(np.uint8).reshape(k // 512, 16, n))


def unpack_weight(words, scales, fmt):
    g, p, n, _ = words.shape
    if fmt == "e4m3":
        vals = np.ascontiguousarray(words).view(ml_dtypes.float8_e4m3fn).astype(np.float64)
    else:
        nib = np.empty((g, p, n, 4), np.uint8)
        nib[..., 0::2] = words & 0xF
        nib[..., 1::2] = words >> 4
        vals = E2M1[nib]
    vals = vals * np.repeat(np.exp2(scales.astype(np.float64) - 127.0), 8, axis=1)[..., None]
    return vals.transpose(0, 1, 3, 2).reshape(g * 512, n)


B, F, DOF, N_CLS = 256, 256, 64, 1024
K = F * DOF
FMT = "e4m3"


def setup_inputs():
    s = mx_kscale(K)
    c = s.max() / s.min()
    far = (s.reshape(F, 2, 32)[:, :, 0] == s.max()) & (c > 1.0)
    far[:, 1] &= ~far[:, 0]
    lo, hi = -3.0 / c, 3.0
    pos = 0.5 + np.random.standard_normal((B, F)) / 6.0
    pos = np.where(far[:, 1], 0.48 * np.minimum(pos, 1.0), pos)
    pos = np.where(far[:, 0], 1.0 - 0.48 * (1.0 - np.maximum(pos, 0.0)), pos)
    xv = f64(bf(lo + (hi - lo) * pos))
    xv[xv == hi] = 2.5
    xv[xv == lo] = -2.5
    wf = (np.where(far, c, 1.0)[:, :, None] * np.ones(32)).reshape(K)
    w_nk = np.random.standard_normal((N_CLS, K)) * 0.005 * wf
    words, scales = pack_weight(np.ascontiguousarray(w_nk.T), FMT)
    return {"x": bf(xv), "min_x": bf(np.array([lo])), "max_x": bf(np.array([hi])),
            "W_words": words, "W_scales": scales, "dof": DOF}


def _lagrange_embed(x, min_x, max_x, dof):
    b_, f_ = x.shape
    T = dof - 1
    h = 1.0 / T
    xn = ((x.reshape(-1, 1) - min_x) / (max_x - min_x)).reshape(-1)
    t = np.arange(T, dtype=np.float64)
    s = xn[:, None] / h
    lam0 = s - t
    lam1 = (t + 1.0) - s
    n2t = ((lam0 >= 0.0) & (lam1 >= 0.0)).astype(np.float64)
    z = np.zeros((xn.shape[0], 1), dtype=np.float64)
    mask = np.concatenate([n2t, z], axis=1) + np.concatenate([z, n2t], axis=1)
    w0 = n2t * lam0
    w1 = n2t * lam1
    shape_vals = np.concatenate([w1, z], axis=1) + np.concatenate([z, w0], axis=1)
    basis = shape_vals / np.maximum(mask, 1.0)
    emb = basis * (max_x - min_x) + min_x
    return emb.reshape(b_, f_ * dof)


def reference(x, min_x, max_x, W_words, W_scales, dof):
    emb = _lagrange_embed(f64(x), f64(min_x), f64(max_x), int(dof))
    return mxq(emb, 1, "e4m3") @ unpack_weight(W_words, W_scales, FMT)

@@ -1,0 +1,240 @@
+from contextlib import ExitStack
+
+import concourse.masks as masks
+import concourse.mybir as mybir
+
+FP8X4 = mybir.dt.float8_e4m3fn_x4
+BF16 = mybir.dt.bfloat16
+F32 = mybir.dt.float32
+I32 = mybir.dt.int32
+U32 = mybir.dt.uint32
+U8 = mybir.dt.uint8
+ALU = mybir.AluOpType
+ACTF = mybir.ActivationFunctionType
+
+P = 128
+B = 256
+F = 256
+DOF = 64
+N = 1024
+K = F * DOF
+GROUPS = K // 512
+SETS = 4
+PER_SET = GROUPS // SETS
+FLOPS = 2 * B * K * N
+
+
+def tile_lagrangenet_kernel(tc, x, min_x, max_x, W_words, W_scales, dof, out):
+    nc = tc.nc
+    assert dof == DOF
+    with ExitStack() as ctx:
+        const = ctx.enter_context(tc.tile_pool(name="const", bufs=1))
+        wpool = ctx.enter_context(tc.tile_pool(name="wpool", bufs=16))
+        upool = ctx.enter_context(tc.tile_pool(name="upool", bufs=3))
+        gpool = ctx.enter_context(tc.tile_pool(name="gpool", bufs=3))
+        cpool = ctx.enter_context(tc.tile_pool(name="cpool", bufs=4))
+        opool = ctx.enter_context(tc.tile_pool(name="opool", bufs=4))
+        accp = ctx.enter_context(tc.psum_pool(name="accp", bufs=1))
+        bcp = ctx.enter_context(tc.psum_pool(name="bcp", bufs=3))
+        tpp = ctx.enter_context(tc.psum_pool(name="tpp", bufs=1))
+
+        ctx.enter_context(tc.manual_schedule())
+        n_units = GROUPS // 2
+
+        x_sb = const.tile([P, 2, F], BF16)
+        nc.scalar.dma_start(out=x_sb[:], in_=x.rearrange("(h p) f -> p h f", p=P))
+        mn_b = const.tile([P, 1], BF16)
+        nc.scalar.dma_start(out=mn_b[:], in_=min_x.partition_broadcast(P))
+        mx_b = const.tile([P, 1], BF16)
+        nc.scalar.dma_start(out=mx_b[:], in_=max_x.partition_broadcast(P))
+
+        warm = const.tile([P, 1], F32)
+        nc.vector.memset(warm[:], 0.0)
+
+        wsc = const.tile([P, PER_SET, N], U8, align_bytes=64)
+        nc.vector.memset(wsc[:].rearrange("p c n -> p (c n)").bitcast(I32), 0)
+
+        w_view = W_words.bitcast(I32).rearrange("g p n o -> p g (n o)")
+        s_view = W_scales.bitcast(I32).rearrange("(c j) (q r) n -> q r j c n", j=SETS, r=4)
+
+        def load_scales(c_lo, c_hi):
+            for q in range(4):
+                for r in range(4):
+                    nc.sync.dma_start(
+                        out=wsc[32 * q + r : 32 * q + 16 : 4, c_lo:c_hi, :].bitcast(I32),
+                        in_=s_view[q, r][:, c_lo:c_hi, :],
+                    )
+
+        w_tiles = []
+        for u in range(n_units):
+            w_t = wpool.tile([P, 2, N], U32, align_bytes=64)
+            w_tiles.append(w_t)
+            if u == 0:
+                nc.sync.dma_start(out=w_t[:, 0:1, :].bitcast(I32), in_=w_view[:, 0:1, :])
+                load_scales(0, 2)
+                nc.sync.dma_start(out=w_t[:, 1:2, :].bitcast(I32), in_=w_view[:, 1:2, :])
+            else:
+                if u == 3:
+                    load_scales(2, PER_SET)
+                nc.sync.dma_start(out=w_t[:].bitcast(I32), in_=w_view[:, 2 * u : 2 * u + 2, :])
+
+        warm2 = const.tile([P, 1], F32)
+        nc.scalar.activation(out=warm2[:], in_=warm[:], func=ACTF.Abs)
+
+        ident = const.tile([P, P], BF16)
+        masks.make_identity(nc, ident[:])
+        p_int = const.tile([P, 4], I32)
+        nc.gpsimd.iota(p_int[:], pattern=[[1, 4]], base=0, channel_multiplier=4)
+
+        rep = const.tile([P, 16 * P], BF16)
+        for b4 in range(4):
+            nc.scalar.copy(
+                out=rep[:, 512 * b4 : 512 * b4 + 512].rearrange("p (f r) -> p f r", r=16),
+                in_=ident[:, 32 * b4 : 32 * b4 + 32].unsqueeze(2).to_broadcast([P, 32, 16]),
+            )
+
+        p_and = const.tile([P, 4], I32)
+        nc.vector.tensor_single_scalar(out=p_and[:], in_=p_int[:], scalar=DOF - 1, op=ALU.bitwise_and)
+        p_f = const.tile([P, 4], F32)
+        nc.vector.tensor_copy(out=p_f[:], in_=p_and[:])
+
+        cst = const.tile([P, 8], F32)
+        mn = cst[:, 0:1]
+        mx = cst[:, 1:2]
+        rng = cst[:, 2:3]
+        nrng = cst[:, 3:4]
+        c63 = cst[:, 4:5]
+        nmn = cst[:, 5:6]
+        nc.vector.tensor_copy(out=mn, in_=mn_b[:])
+        nc.vector.tensor_copy(out=mx, in_=mx_b[:])
+        nc.vector.tensor_sub(out=rng, in0=mx, in1=mn)
+        nc.vector.tensor_sub(out=nrng, in0=mn, in1=mx)
+        nc.vector.tensor_scalar_mul(out=c63, in0=mn, scalar1=-float(DOF - 1))
+        nc.vector.tensor_scalar_mul(out=nmn, in0=mn, scalar1=-1.0)
+        nbias = const.tile([P, 4], F32)
+        nc.vector.tensor_scalar(
+            out=nbias[:], in0=p_f[:], scalar1=nrng, scalar2=c63, op0=ALU.mult, op1=ALU.add
+        )
+
+        xt_ps = tpp.tile([P, 2, B], BF16)
+        for hf in range(2):
+            for h in range(2):
+                nc.tensor.transpose(
+                    xt_ps[:, hf, P * h : P * h + P], x_sb[:, h, P * hf : P * hf + P], ident[:]
+                )
+        xm = const.tile([P, 2, B], BF16)
+
+        def push_outside(hf):
+            below = const.tile([P, B], F32, name="below%d" % hf)
+            nc.vector.tensor_scalar(
+                out=below[:], in0=xt_ps[:, hf, :], scalar1=mn, scalar2=None, op0=ALU.is_lt
+            )
+            side = const.tile([P, B], F32, name="side%d" % hf)
+            nc.vector.scalar_tensor_tensor(
+                out=side[:], in0=xt_ps[:, hf, :], scalar=mx, in1=below[:], op0=ALU.is_gt, op1=ALU.subtract
+            )
+            nc.vector.scalar_tensor_tensor(
+                out=xm[:, hf, :], in0=side[:], scalar=rng, in1=xt_ps[:, hf, :], op0=ALU.mult, op1=ALU.add
+            )
+
+        push_outside(0)
+
+        acc = [
+            [accp.tile([P, 512], F32, name="acc%d%d" % (h, nh)) for nh in range(2)] for h in range(2)
+        ]
+
+        bc_tiles = {}
+
+        def spread(u):
+            bc = bcp.tile([P, 512], F32, name="bc")
+            bc_tiles[u] = bc
+            for gg in range(2):
+                g = 2 * u + gg
+                nc.tensor.matmul(
+                    bc[:, B * gg : B * gg + B],
+                    lhsT=rep[:, P * (g % 16) : P * (g % 16) + P],
+                    rhs=xm[:, g // 16, :],
+                    start=True,
+                    stop=True,
+                )
+
+        def mx_pass(u, gg, h, nh, codes, plane):
+            g = 2 * u + gg
+            first = u == 0 and gg == 0
+            last = u == n_units - 1 and gg == 1
+            cols = slice(B * gg + P * h, B * gg + P * h + P)
+            nc.tensor.matmul_mx(
+                out=acc[h][nh][:],
+                lhsT=codes[:, cols].bitcast(FP8X4),
+                lhsT_scale=plane[:, cols],
+                rhs=w_tiles[u][:, gg, 512 * nh : 512 * nh + 512].bitcast(FP8X4),
+                rhs_scale=wsc[4 * (g % 4) : P, g // 4, 512 * nh : 512 * nh + 512],
+                start=first,
+                stop=last,
+            )
+
+        for u in range(3):
+            spread(u)
+
+        for u in range(n_units):
+            bc = bc_tiles[u]
+            u_t = upool.tile([P, 4, 512], F32)
+            pieces = [(0, 256), (256, 512)] if u == 0 else [(0, 512)]
+            for lo, hi in pieces:
+                for t in range(4):
+                    nc.scalar.activation(
+                        out=u_t[:, t, lo:hi],
+                        in_=bc[:, lo:hi],
+                        func=ACTF.Abs,
+                        bias=nbias[:, t : t + 1],
+                        scale=float(DOF - 1),
+                    )
+            if u == 2:
+                push_outside(1)
+            g_t = gpool.tile([P, 512, 4], BF16, align_bytes=64)
+            codes = cpool.tile([P, 512], U32, align_bytes=64)
+            plane = cpool.tile([P, 512], U8, align_bytes=64)
+            for gg in range(2):
+                nc.vector.tensor_scalar(
+                    out=g_t[:, B * gg : B * gg + B, :],
+                    in0=u_t[:, :, B * gg : B * gg + B].rearrange("p t c -> p c t"),
+                    scalar1=mx,
+                    scalar2=nmn,
+                    op0=ALU.subtract,
+                    op1=ALU.min,
+                )
+                if u == 0:
+                    nc.vector.quantize_mx(
+                        out=codes[:, B * gg : B * gg + B].bitcast(FP8X4),
+                        scales=plane[:, B * gg : B * gg + B],
+                        in_=g_t[:, B * gg : B * gg + B, :].rearrange("p c t -> p (c t)"),
+                    )
+            if u > 0:
+                for gg in range(2):
+                    nc.vector.quantize_mx(
+                        out=codes[:, B * gg : B * gg + B].bitcast(FP8X4),
+                        scales=plane[:, B * gg : B * gg + B],
+                        in_=g_t[:, B * gg : B * gg + B, :].rearrange("p c t -> p (c t)"),
+                    )
+            if u + 3 < n_units:
+                spread(u + 3)
+            if u < n_units - 1:
+                for gg in range(2):
+                    for h in range(2):
+                        for nh in range(2):
+                            mx_pass(u, gg, h, nh, codes, plane)
+            else:
+                k = 0
+                for h in range(2):
+                    for nh in range(2):
+                        for gg in range(2):
+                            mx_pass(u, gg, h, nh, codes, plane)
+                        o_t = opool.tile([P, 512], F32)
+                        if k % 2 == 0:
+                            nc.scalar.mul(out=o_t[:], in_=acc[h][nh][:], mul=-1.0)
+                        else:
+                            nc.vector.tensor_scalar_mul(out=o_t[:], in0=acc[h][nh][:], scalar1=-1.0)
+                        nc.sync.dma_start(
+                            out=out[P * h : P * h + P, 512 * nh : 512 * nh + 512], in_=o_t[:]
+                        )
+                        k += 1

@@ -39,7 +39,8 @@ def tile_lagrangenet_kernel(tc, x, min_x, max_x, W_words, W_scales, dof, out):
         tpp = ctx.enter_context(tc.psum_pool(name="tpp", bufs=1))
 
         ctx.enter_context(tc.manual_schedule())
-        n_units = GROUPS // 2
+        units = [(j, c0) for j in range(SETS) for c0 in range(0, PER_SET, 2)]
+        n_units = len(units)
 
         x_sb = const.tile([P, 2, F], BF16)
         nc.scalar.dma_start(out=x_sb[:], in_=x.rearrange("(h p) f -> p h f", p=P))
@@ -54,29 +55,26 @@ def tile_lagrangenet_kernel(tc, x, min_x, max_x, W_words, W_scales, dof, out):
         wsc = const.tile([P, PER_SET, N], U8, align_bytes=64)
         nc.vector.memset(wsc[:].rearrange("p c n -> p (c n)").bitcast(I32), 0)
 
-        w_view = W_words.bitcast(I32).rearrange("g p n o -> p g (n o)")
-        s_view = W_scales.bitcast(I32).rearrange("(c j) (q r) n -> q r j c n", j=SETS, r=4)
+        w_view = W_words.bitcast(I32).rearrange("(c j) p n o -> j p c (n o)", j=SETS)
+        s_view = W_scales.bitcast(I32).rearrange("(c j) (q r) n -> j r q c n", j=SETS, r=4)
 
-        def load_scales(c_lo, c_hi):
-            for q in range(4):
-                for r in range(4):
-                    nc.sync.dma_start(
-                        out=wsc[32 * q + r : 32 * q + 16 : 4, c_lo:c_hi, :].bitcast(I32),
-                        in_=s_view[q, r][:, c_lo:c_hi, :],
-                    )
+        def load_scales(j):
+            for r in range(4):
+                nc.sync.dma_start(out=wsc[4 * j + r : P : 32, :, :].bitcast(I32), in_=s_view[j, r])
 
         w_tiles = []
         for u in range(n_units):
+            j, c0 = units[u]
             w_t = wpool.tile([P, 2, N], U32, align_bytes=64)
             w_tiles.append(w_t)
             if u == 0:
-                nc.sync.dma_start(out=w_t[:, 0:1, :].bitcast(I32), in_=w_view[:, 0:1, :])
-                load_scales(0, 2)
-                nc.sync.dma_start(out=w_t[:, 1:2, :].bitcast(I32), in_=w_view[:, 1:2, :])
+                nc.sync.dma_start(out=w_t[:, 0:1, :].bitcast(I32), in_=w_view[j][:, c0 : c0 + 1, :])
+                load_scales(0)
+                nc.sync.dma_start(out=w_t[:, 1:2, :].bitcast(I32), in_=w_view[j][:, c0 + 1 : c0 + 2, :])
             else:
-                if u == 3:
-                    load_scales(2, PER_SET)
-                nc.sync.dma_start(out=w_t[:].bitcast(I32), in_=w_view[:, 2 * u : 2 * u + 2, :])
+                if c0 == 2 and j + 1 < SETS:
+                    load_scales(j + 1)
+                nc.sync.dma_start(out=w_t[:].bitcast(I32), in_=w_view[j][:, c0 : c0 + 2, :])
 
         warm2 = const.tile([P, 1], F32)
         nc.scalar.activation(out=warm2[:], in_=warm[:], func=ACTF.Abs)
@@ -89,8 +87,11 @@ def tile_lagrangenet_kernel(tc, x, min_x, max_x, W_words, W_scales, dof, out):
         rep = const.tile([P, 16 * P], BF16)
         for b4 in range(4):
             nc.scalar.copy(
-                out=rep[:, 512 * b4 : 512 * b4 + 512].rearrange("p (f r) -> p f r", r=16),
-                in_=ident[:, 32 * b4 : 32 * b4 + 32].unsqueeze(2).to_broadcast([P, 32, 16]),
+                out=rep[:].rearrange("p (a b f r) -> p b a f r", a=4, b=4, f=8, r=16)[:, b4],
+                in_=ident[:]
+                .rearrange("p (a b f) -> p b a f", a=4, b=4, f=8)[:, b4]
+                .unsqueeze(3)
+                .to_broadcast([P, 4, 8, 16]),
             )
 
         p_and = const.tile([P, 4], I32)
@@ -138,6 +139,7 @@ def tile_lagrangenet_kernel(tc, x, min_x, max_x, W_words, W_scales, dof, out):
             )
 
         push_outside(0)
+        push_outside(1)
 
         acc = [
             [accp.tile([P, 512], F32, name="acc%d%d" % (h, nh)) for nh in range(2)] for h in range(2)
@@ -146,10 +148,11 @@ def tile_lagrangenet_kernel(tc, x, min_x, max_x, W_words, W_scales, dof, out):
         bc_tiles = {}
 
         def spread(u):
+            j, c0 = units[u]
             bc = bcp.tile([P, 512], F32, name="bc")
             bc_tiles[u] = bc
             for gg in range(2):
-                g = 2 * u + gg
+                g = 4 * (c0 + gg) + j
                 nc.tensor.matmul(
                     bc[:, B * gg : B * gg + B],
                     lhsT=rep[:, P * (g % 16) : P * (g % 16) + P],
@@ -159,7 +162,7 @@ def tile_lagrangenet_kernel(tc, x, min_x, max_x, W_words, W_scales, dof, out):
                 )
 
         def mx_pass(u, gg, h, nh, codes, plane):
-            g = 2 * u + gg
+            j, c0 = units[u]
             first = u == 0 and gg == 0
             last = u == n_units - 1 and gg == 1
             cols = slice(B * gg + P * h, B * gg + P * h + P)
@@ -168,7 +171,7 @@ def tile_lagrangenet_kernel(tc, x, min_x, max_x, W_words, W_scales, dof, out):
                 lhsT=codes[:, cols].bitcast(FP8X4),
                 lhsT_scale=plane[:, cols],
                 rhs=w_tiles[u][:, gg, 512 * nh : 512 * nh + 512].bitcast(FP8X4),
-                rhs_scale=wsc[4 * (g % 4) : P, g // 4, 512 * nh : 512 * nh + 512],
+                rhs_scale=wsc[4 * j : P, c0 + gg, 512 * nh : 512 * nh + 512],
                 start=first,
                 stop=last,
             )
@@ -189,8 +192,6 @@ def tile_lagrangenet_kernel(tc, x, min_x, max_x, W_words, W_scales, dof, out):
                         bias=nbias[:, t : t + 1],
                         scale=float(DOF - 1),
                     )
-            if u == 2:
-                push_outside(1)
             g_t = gpool.tile([P, 512, 4], BF16, align_bytes=64)
             codes = cpool.tile([P, 512], U32, align_bytes=64)
             plane = cpool.tile([P, 512], U8, align_bytes=64)

@@ -39,8 +39,7 @@ def tile_lagrangenet_kernel(tc, x, min_x, max_x, W_words, W_scales, dof, out):
         tpp = ctx.enter_context(tc.psum_pool(name="tpp", bufs=1))
 
         ctx.enter_context(tc.manual_schedule())
-        units = [(j, c0) for j in range(SETS) for c0 in range(0, PER_SET, 2)]
-        n_units = len(units)
+        n_units = GROUPS // 2
 
         x_sb = const.tile([P, 2, F], BF16)
         nc.scalar.dma_start(out=x_sb[:], in_=x.rearrange("(h p) f -> p h f", p=P))
@@ -55,26 +54,27 @@ def tile_lagrangenet_kernel(tc, x, min_x, max_x, W_words, W_scales, dof, out):
         wsc = const.tile([P, PER_SET, N], U8, align_bytes=64)
         nc.vector.memset(wsc[:].rearrange("p c n -> p (c n)").bitcast(I32), 0)
 
-        w_view = W_words.bitcast(I32).rearrange("(c j) p n o -> j p c (n o)", j=SETS)
-        s_view = W_scales.bitcast(I32).rearrange("(c j) (q r) n -> j r q c n", j=SETS, r=4)
+        w_view = W_words.bitcast(I32).rearrange("g p n o -> p g (n o)")
+        s_view = W_scales.bitcast(I32).rearrange("(c j) (q r) n -> q r j c n", j=SETS, r=4)
 
-        def load_scales(j):
-            for r in range(4):
-                nc.sync.dma_start(out=wsc[4 * j + r : P : 32, :, :].bitcast(I32), in_=s_view[j, r])
+        def load_scales(c_lo, c_hi):
+            for q in range(4):
+                for r in range(4):
+                    nc.sync.dma_start(
+                        out=wsc[32 * q + r : 32 * q + 16 : 4, c_lo:c_hi, :].bitcast(I32),
+                        in_=s_view[q, r][:, c_lo:c_hi, :],
+                    )
 
         w_tiles = []
         for u in range(n_units):
-            j, c0 = units[u]
             w_t = wpool.tile([P, 2, N], U32, align_bytes=64)
             w_tiles.append(w_t)
             if u == 0:
-                nc.sync.dma_start(out=w_t[:, 0:1, :].bitcast(I32), in_=w_view[j][:, c0 : c0 + 1, :])
-                load_scales(0)
-                nc.sync.dma_start(out=w_t[:, 1:2, :].bitcast(I32), in_=w_view[j][:, c0 + 1 : c0 + 2, :])
+                nc.sync.dma_start(out=w_t[:, 0:1, :].bitcast(I32), in_=w_view[:, 0:1, :])
+                load_scales(0, PER_SET)
+                nc.sync.dma_start(out=w_t[:, 1:2, :].bitcast(I32), in_=w_view[:, 1:2, :])
             else:
-                if c0 == 2 and j + 1 < SETS:
-                    load_scales(j + 1)
-                nc.sync.dma_start(out=w_t[:].bitcast(I32), in_=w_view[j][:, c0 : c0 + 2, :])
+                nc.sync.dma_start(out=w_t[:].bitcast(I32), in_=w_view[:, 2 * u : 2 * u + 2, :])
 
         warm2 = const.tile([P, 1], F32)
         nc.scalar.activation(out=warm2[:], in_=warm[:], func=ACTF.Abs)
@@ -87,11 +87,8 @@ def tile_lagrangenet_kernel(tc, x, min_x, max_x, W_words, W_scales, dof, out):
         rep = const.tile([P, 16 * P], BF16)
         for b4 in range(4):
             nc.scalar.copy(
-                out=rep[:].rearrange("p (a b f r) -> p b a f r", a=4, b=4, f=8, r=16)[:, b4],
-                in_=ident[:]
-                .rearrange("p (a b f) -> p b a f", a=4, b=4, f=8)[:, b4]
-                .unsqueeze(3)
-                .to_broadcast([P, 4, 8, 16]),
+                out=rep[:, 512 * b4 : 512 * b4 + 512].rearrange("p (f r) -> p f r", r=16),
+                in_=ident[:, 32 * b4 : 32 * b4 + 32].unsqueeze(2).to_broadcast([P, 32, 16]),
             )
 
         p_and = const.tile([P, 4], I32)
@@ -139,7 +136,6 @@ def tile_lagrangenet_kernel(tc, x, min_x, max_x, W_words, W_scales, dof, out):
             )
 
         push_outside(0)
-        push_outside(1)
 
         acc = [
             [accp.tile([P, 512], F32, name="acc%d%d" % (h, nh)) for nh in range(2)] for h in range(2)
@@ -148,11 +144,10 @@ def tile_lagrangenet_kernel(tc, x, min_x, max_x, W_words, W_scales, dof, out):
         bc_tiles = {}
 
         def spread(u):
-            j, c0 = units[u]
             bc = bcp.tile([P, 512], F32, name="bc")
             bc_tiles[u] = bc
             for gg in range(2):
-                g = 4 * (c0 + gg) + j
+                g = 2 * u + gg
                 nc.tensor.matmul(
                     bc[:, B * gg : B * gg + B],
                     lhsT=rep[:, P * (g % 16) : P * (g % 16) + P],
@@ -162,7 +157,7 @@ def tile_lagrangenet_kernel(tc, x, min_x, max_x, W_words, W_scales, dof, out):
                 )
 
         def mx_pass(u, gg, h, nh, codes, plane):
-            j, c0 = units[u]
+            g = 2 * u + gg
             first = u == 0 and gg == 0
             last = u == n_units - 1 and gg == 1
             cols = slice(B * gg + P * h, B * gg + P * h + P)
@@ -171,7 +166,7 @@ def tile_lagrangenet_kernel(tc, x, min_x, max_x, W_words, W_scales, dof, out):
                 lhsT=codes[:, cols].bitcast(FP8X4),
                 lhsT_scale=plane[:, cols],
                 rhs=w_tiles[u][:, gg, 512 * nh : 512 * nh + 512].bitcast(FP8X4),
-                rhs_scale=wsc[4 * j : P, c0 + gg, 512 * nh : 512 * nh + 512],
+                rhs_scale=wsc[4 * (g % 4) : P, g // 4, 512 * nh : 512 * nh + 512],
                 start=first,
                 stop=last,
             )
@@ -192,6 +187,8 @@ def tile_lagrangenet_kernel(tc, x, min_x, max_x, W_words, W_scales, dof, out):
                         bias=nbias[:, t : t + 1],
                         scale=float(DOF - 1),
                     )
+            if u == 2:
+                push_outside(1)
             g_t = gpool.tile([P, 512, 4], BF16, align_bytes=64)
             codes = cpool.tile([P, 512], U32, align_bytes=64)
             plane = cpool.tile([P, 512], U8, align_bytes=64)

@@ -21,6 +21,8 @@ K = F * DOF
 GROUPS = K // 512
 SETS = 4
 PER_SET = GROUPS // SETS
+UNITS = GROUPS // 2
+BANKS = GROUPS // 4
 FLOPS = 2 * B * K * N
 
 
@@ -29,17 +31,14 @@ def tile_lagrangenet_kernel(tc, x, min_x, max_x, W_words, W_scales, dof, out):
     assert dof == DOF
     with ExitStack() as ctx:
         const = ctx.enter_context(tc.tile_pool(name="const", bufs=1))
-        wpool = ctx.enter_context(tc.tile_pool(name="wpool", bufs=16))
+        wpool = ctx.enter_context(tc.tile_pool(name="wpool", bufs=UNITS))
         upool = ctx.enter_context(tc.tile_pool(name="upool", bufs=3))
         gpool = ctx.enter_context(tc.tile_pool(name="gpool", bufs=3))
         cpool = ctx.enter_context(tc.tile_pool(name="cpool", bufs=4))
         opool = ctx.enter_context(tc.tile_pool(name="opool", bufs=4))
         accp = ctx.enter_context(tc.psum_pool(name="accp", bufs=1))
-        bcp = ctx.enter_context(tc.psum_pool(name="bcp", bufs=3))
-        tpp = ctx.enter_context(tc.psum_pool(name="tpp", bufs=1))
-
+        bcp = ctx.enter_context(tc.psum_pool(name="bcp", bufs=4))
         ctx.enter_context(tc.manual_schedule())
-        n_units = GROUPS // 2
 
         x_sb = const.tile([P, 2, F], BF16)
         nc.scalar.dma_start(out=x_sb[:], in_=x.rearrange("(h p) f -> p h f", p=P))
@@ -53,26 +52,22 @@ def tile_lagrangenet_kernel(tc, x, min_x, max_x, W_words, W_scales, dof, out):
 
         wsc = const.tile([P, PER_SET, N], U8, align_bytes=64)
         nc.vector.memset(wsc[:].rearrange("p c n -> p (c n)").bitcast(I32), 0)
-
         w_view = W_words.bitcast(I32).rearrange("g p n o -> p g (n o)")
         s_view = W_scales.bitcast(I32).rearrange("(c j) (q r) n -> q r j c n", j=SETS, r=4)
 
-        def load_scales(c_lo, c_hi):
-            for q in range(4):
-                for r in range(4):
-                    nc.sync.dma_start(
-                        out=wsc[32 * q + r : 32 * q + 16 : 4, c_lo:c_hi, :].bitcast(I32),
-                        in_=s_view[q, r][:, c_lo:c_hi, :],
-                    )
-
         w_tiles = []
-        for u in range(n_units):
+        for u in range(UNITS):
             w_t = wpool.tile([P, 2, N], U32, align_bytes=64)
             w_tiles.append(w_t)
-            if u == 0:
-                nc.sync.dma_start(out=w_t[:, 0:1, :].bitcast(I32), in_=w_view[:, 0:1, :])
-                load_scales(0, PER_SET)
-                nc.sync.dma_start(out=w_t[:, 1:2, :].bitcast(I32), in_=w_view[:, 1:2, :])
+            if u == 0 or u == UNITS - 1:
+                nc.sync.dma_start(out=w_t[:, 0:1, :].bitcast(I32), in_=w_view[:, 2 * u : 2 * u + 1, :])
+                if u == 0:
+                    for q in range(4):
+                        for r in range(4):
+                            nc.sync.dma_start(
+                                out=wsc[32 * q + r : 32 * q + 16 : 4, :, :].bitcast(I32), in_=s_view[q, r]
+                            )
+                nc.sync.dma_start(out=w_t[:, 1:2, :].bitcast(I32), in_=w_view[:, 2 * u + 1 : 2 * u + 2, :])
             else:
                 nc.sync.dma_start(out=w_t[:].bitcast(I32), in_=w_view[:, 2 * u : 2 * u + 2, :])
 
@@ -85,57 +80,75 @@ def tile_lagrangenet_kernel(tc, x, min_x, max_x, W_words, W_scales, dof, out):
         nc.gpsimd.iota(p_int[:], pattern=[[1, 4]], base=0, channel_multiplier=4)
 
         rep = const.tile([P, 16 * P], BF16)
-        for b4 in range(4):
-            nc.scalar.copy(
-                out=rep[:, 512 * b4 : 512 * b4 + 512].rearrange("p (f r) -> p f r", r=16),
-                in_=ident[:, 32 * b4 : 32 * b4 + 32].unsqueeze(2).to_broadcast([P, 32, 16]),
+
+        def rep_views(b4):
+            return (
+                rep[:, 512 * b4 : 512 * b4 + 512].rearrange("p (f r) -> p f r", r=16),
+                ident[:, 32 * b4 : 32 * b4 + 32].unsqueeze(2).to_broadcast([P, 32, 16]),
             )
+
+        dst, src = rep_views(0)
+        nc.vector.tensor_copy(out=dst, in_=src)
+        dst, src = rep_views(1)
+        nc.scalar.copy(out=dst, in_=src)
+        for b4 in range(2, 4):
+            dst, src = rep_views(b4)
+            nc.gpsimd.tensor_scalar(out=dst, in0=src, scalar1=1.0, scalar2=0.0, op0=ALU.mult, op1=ALU.add)
 
         p_and = const.tile([P, 4], I32)
         nc.vector.tensor_single_scalar(out=p_and[:], in_=p_int[:], scalar=DOF - 1, op=ALU.bitwise_and)
         p_f = const.tile([P, 4], F32)
         nc.vector.tensor_copy(out=p_f[:], in_=p_and[:])
 
-        cst = const.tile([P, 8], F32)
-        mn = cst[:, 0:1]
-        mx = cst[:, 1:2]
-        rng = cst[:, 2:3]
-        nrng = cst[:, 3:4]
-        c63 = cst[:, 4:5]
-        nmn = cst[:, 5:6]
-        nc.vector.tensor_copy(out=mn, in_=mn_b[:])
-        nc.vector.tensor_copy(out=mx, in_=mx_b[:])
-        nc.vector.tensor_sub(out=rng, in0=mx, in1=mn)
-        nc.vector.tensor_sub(out=nrng, in0=mn, in1=mx)
-        nc.vector.tensor_scalar_mul(out=c63, in0=mn, scalar1=-float(DOF - 1))
-        nc.vector.tensor_scalar_mul(out=nmn, in0=mn, scalar1=-1.0)
+        cst = const.tile([P, 4], F32)
+        rng = cst[:, 0:1]
+        nrng = cst[:, 1:2]
+        c63 = cst[:, 2:3]
+        nc.vector.tensor_sub(out=nrng, in0=mn_b[:], in1=mx_b[:])
+        nc.vector.tensor_scalar_mul(out=c63, in0=mn_b[:], scalar1=-float(DOF - 1))
         nbias = const.tile([P, 4], F32)
         nc.vector.tensor_scalar(
             out=nbias[:], in0=p_f[:], scalar1=nrng, scalar2=c63, op0=ALU.mult, op1=ALU.add
         )
+        nc.vector.tensor_sub(out=rng, in0=mx_b[:], in1=mn_b[:])
+        nmn_b = const.tile([P, 1], BF16)
 
-        xt_ps = tpp.tile([P, 2, B], BF16)
+        xt_ps = bcp.tile([P, 2, B], BF16, tag="bc")
         for hf in range(2):
             for h in range(2):
                 nc.tensor.transpose(
                     xt_ps[:, hf, P * h : P * h + P], x_sb[:, h, P * hf : P * hf + P], ident[:]
                 )
+
+        def spread_group(dst_ps, g, rhs):
+            nc.tensor.matmul(
+                dst_ps, lhsT=rep[:, P * (g % 16) : P * (g % 16) + P], rhs=rhs, start=True, stop=True
+            )
+
         xm = const.tile([P, 2, B], BF16)
-
-        def push_outside(hf):
-            below = const.tile([P, B], F32, name="below%d" % hf)
+        below = const.tile([P, 2, B], F32)
+        side = const.tile([P, 2, B], F32)
+        for hf in range(2):
             nc.vector.tensor_scalar(
-                out=below[:], in0=xt_ps[:, hf, :], scalar1=mn, scalar2=None, op0=ALU.is_lt
-            )
-            side = const.tile([P, B], F32, name="side%d" % hf)
-            nc.vector.scalar_tensor_tensor(
-                out=side[:], in0=xt_ps[:, hf, :], scalar=mx, in1=below[:], op0=ALU.is_gt, op1=ALU.subtract
+                out=below[:, hf, :], in0=xt_ps[:, hf, :], scalar1=mn_b[:], scalar2=None, op0=ALU.is_lt
             )
             nc.vector.scalar_tensor_tensor(
-                out=xm[:, hf, :], in0=side[:], scalar=rng, in1=xt_ps[:, hf, :], op0=ALU.mult, op1=ALU.add
+                out=side[:, hf, :],
+                in0=xt_ps[:, hf, :],
+                scalar=mx_b[:],
+                in1=below[:, hf, :],
+                op0=ALU.is_gt,
+                op1=ALU.subtract,
             )
-
-        push_outside(0)
+            nc.vector.scalar_tensor_tensor(
+                out=xm[:, hf, :],
+                in0=side[:, hf, :],
+                scalar=rng,
+                in1=xt_ps[:, hf, :],
+                op0=ALU.mult,
+                op1=ALU.add,
+            )
+        nc.vector.tensor_scalar_mul(out=nmn_b[:], in0=mn_b[:], scalar1=-1.0)
 
         acc = [
             [accp.tile([P, 512], F32, name="acc%d%d" % (h, nh)) for nh in range(2)] for h in range(2)
@@ -143,96 +156,85 @@ def tile_lagrangenet_kernel(tc, x, min_x, max_x, W_words, W_scales, dof, out):
 
         bc_tiles = {}
 
-        def spread(u):
-            bc = bcp.tile([P, 512], F32, name="bc")
-            bc_tiles[u] = bc
-            for gg in range(2):
-                g = 2 * u + gg
-                nc.tensor.matmul(
-                    bc[:, B * gg : B * gg + B],
-                    lhsT=rep[:, P * (g % 16) : P * (g % 16) + P],
-                    rhs=xm[:, g // 16, :],
-                    start=True,
-                    stop=True,
-                )
+        def spread(k):
+            bc = bcp.tile([P, 4 * B], BF16, tag="bc")
+            bc_tiles[k] = bc
+            for gg in range(4):
+                g = 4 * k + gg
+                spread_group(bc[:, B * gg : B * gg + B], g, xm[:, g // 16, :])
 
-        def mx_pass(u, gg, h, nh, codes, plane):
-            g = 2 * u + gg
-            first = u == 0 and gg == 0
-            last = u == n_units - 1 and gg == 1
-            cols = slice(B * gg + P * h, B * gg + P * h + P)
+        def mx_pass(g, h, nh, codes, plane):
+            cols = slice(B * (g % 2) + P * h, B * (g % 2) + P * h + P)
             nc.tensor.matmul_mx(
                 out=acc[h][nh][:],
                 lhsT=codes[:, cols].bitcast(FP8X4),
                 lhsT_scale=plane[:, cols],
-                rhs=w_tiles[u][:, gg, 512 * nh : 512 * nh + 512].bitcast(FP8X4),
+                rhs=w_tiles[g // 2][:, g % 2, 512 * nh : 512 * nh + 512].bitcast(FP8X4),
                 rhs_scale=wsc[4 * (g % 4) : P, g // 4, 512 * nh : 512 * nh + 512],
-                start=first,
-                stop=last,
+                start=(g == 0),
+                stop=(g == GROUPS - 1),
             )
 
-        for u in range(3):
-            spread(u)
+        for k in range(4):
+            spread(k)
 
-        for u in range(n_units):
-            bc = bc_tiles[u]
+        for u in range(UNITS):
+            bc = bc_tiles[u // 2][:, 512 * (u % 2) : 512 * (u % 2) + 512]
             u_t = upool.tile([P, 4, 512], F32)
-            pieces = [(0, 256), (256, 512)] if u == 0 else [(0, 512)]
-            for lo, hi in pieces:
-                for t in range(4):
-                    nc.scalar.activation(
-                        out=u_t[:, t, lo:hi],
-                        in_=bc[:, lo:hi],
-                        func=ACTF.Abs,
-                        bias=nbias[:, t : t + 1],
-                        scale=float(DOF - 1),
-                    )
-            if u == 2:
-                push_outside(1)
+            for t in range(4):
+                nc.scalar.activation(
+                    out=u_t[:, t, :],
+                    in_=bc,
+                    func=ACTF.Abs,
+                    bias=nbias[:, t : t + 1],
+                    scale=float(DOF - 1),
+                )
             g_t = gpool.tile([P, 512, 4], BF16, align_bytes=64)
             codes = cpool.tile([P, 512], U32, align_bytes=64)
             plane = cpool.tile([P, 512], U8, align_bytes=64)
-            for gg in range(2):
+
+            def finish(gg):
                 nc.vector.tensor_scalar(
                     out=g_t[:, B * gg : B * gg + B, :],
                     in0=u_t[:, :, B * gg : B * gg + B].rearrange("p t c -> p c t"),
-                    scalar1=mx,
-                    scalar2=nmn,
+                    scalar1=mx_b[:],
+                    scalar2=nmn_b[:],
                     op0=ALU.subtract,
                     op1=ALU.min,
                 )
-                if u == 0:
-                    nc.vector.quantize_mx(
-                        out=codes[:, B * gg : B * gg + B].bitcast(FP8X4),
-                        scales=plane[:, B * gg : B * gg + B],
-                        in_=g_t[:, B * gg : B * gg + B, :].rearrange("p c t -> p (c t)"),
-                    )
-            if u > 0:
-                for gg in range(2):
-                    nc.vector.quantize_mx(
-                        out=codes[:, B * gg : B * gg + B].bitcast(FP8X4),
-                        scales=plane[:, B * gg : B * gg + B],
-                        in_=g_t[:, B * gg : B * gg + B, :].rearrange("p c t -> p (c t)"),
-                    )
-            if u + 3 < n_units:
-                spread(u + 3)
-            if u < n_units - 1:
-                for gg in range(2):
-                    for h in range(2):
-                        for nh in range(2):
-                            mx_pass(u, gg, h, nh, codes, plane)
+
+            def quantise(gg):
+                nc.vector.quantize_mx(
+                    out=codes[:, B * gg : B * gg + B].bitcast(FP8X4),
+                    scales=plane[:, B * gg : B * gg + B],
+                    in_=g_t[:, B * gg : B * gg + B, :].rearrange("p c t -> p (c t)"),
+                )
+
+            if u == 0:
+                finish(0)
+                quantise(0)
+                finish(1)
+                quantise(1)
             else:
-                k = 0
+                finish(0)
+                finish(1)
+                quantise(0)
+                quantise(1)
+
+            if u % 2 == 1 and u // 2 + 4 < BANKS:
+                spread(u // 2 + 4)
+
+            for gg in range(2):
+                g = 2 * u + gg
                 for h in range(2):
                     for nh in range(2):
-                        for gg in range(2):
-                            mx_pass(u, gg, h, nh, codes, plane)
-                        o_t = opool.tile([P, 512], F32)
-                        if k % 2 == 0:
-                            nc.scalar.mul(out=o_t[:], in_=acc[h][nh][:], mul=-1.0)
-                        else:
-                            nc.vector.tensor_scalar_mul(out=o_t[:], in0=acc[h][nh][:], scalar1=-1.0)
-                        nc.sync.dma_start(
-                            out=out[P * h : P * h + P, 512 * nh : 512 * nh + 512], in_=o_t[:]
-                        )
-                        k += 1
+                        mx_pass(g, h, nh, codes, plane)
+                        if g == GROUPS - 1:
+                            o_t = opool.tile([P, 512], F32)
+                            if nh == 0:
+                                nc.scalar.mul(out=o_t[:], in_=acc[h][nh][:], mul=-1.0)
+                            else:
+                                nc.vector.tensor_scalar_mul(out=o_t[:], in0=acc[h][nh][:], scalar1=-1.0)
+                            nc.sync.dma_start(
+                                out=out[P * h : P * h + P, 512 * nh : 512 * nh + 512], in_=o_t[:]
+                            )

@@ -67,6 +67,9 @@ def tile_lagrangenet_kernel(tc, x, min_x, max_x, W_words, W_scales, dof, out):
                             nc.sync.dma_start(
                                 out=wsc[32 * q + r : 32 * q + 16 : 4, :, :].bitcast(I32), in_=s_view[q, r]
                             )
+                    for i in range(7):
+                        filler = const.tile([1, 1], BF16, name="filler%d" % i)
+                        nc.sync.dma_start(out=filler[:], in_=min_x.partition_broadcast(1))
                 nc.sync.dma_start(out=w_t[:, 1:2, :].bitcast(I32), in_=w_view[:, 2 * u + 1 : 2 * u + 2, :])
             else:
                 nc.sync.dma_start(out=w_t[:].bitcast(I32), in_=w_view[:, 2 * u : 2 * u + 2, :])

@@ -67,9 +67,6 @@ def tile_lagrangenet_kernel(tc, x, min_x, max_x, W_words, W_scales, dof, out):
                             nc.sync.dma_start(
                                 out=wsc[32 * q + r : 32 * q + 16 : 4, :, :].bitcast(I32), in_=s_view[q, r]
                             )
-                    for i in range(7):
-                        filler = const.tile([1, 1], BF16, name="filler%d" % i)
-                        nc.sync.dma_start(out=filler[:], in_=min_x.partition_broadcast(1))
                 nc.sync.dma_start(out=w_t[:, 1:2, :].bitcast(I32), in_=w_view[:, 2 * u + 1 : 2 * u + 2, :])
             else:
                 nc.sync.dma_start(out=w_t[:].bitcast(I32), in_=w_view[:, 2 * u : 2 * u + 2, :])
@@ -198,8 +195,8 @@ def tile_lagrangenet_kernel(tc, x, min_x, max_x, W_words, W_scales, dof, out):
 
             def finish(gg):
                 nc.vector.tensor_scalar(
-                    out=g_t[:, B * gg : B * gg + B, :],
-                    in0=u_t[:, :, B * gg : B * gg + B].rearrange("p t c -> p c t"),
+                    out=g_t[:, B * gg : B * gg + B, :].rearrange("p c (th tl) -> p th c tl", tl=2),
+                    in0=u_t[:, :, B * gg : B * gg + B].rearrange("p (th tl) c -> p th c tl", tl=2),
                     scalar1=mx_b[:],
                     scalar2=nmn_b[:],
                     op0=ALU.subtract,

@@ -195,8 +195,8 @@ def tile_lagrangenet_kernel(tc, x, min_x, max_x, W_words, W_scales, dof, out):
 
             def finish(gg):
                 nc.vector.tensor_scalar(
-                    out=g_t[:, B * gg : B * gg + B, :].rearrange("p c (th tl) -> p th c tl", tl=2),
-                    in0=u_t[:, :, B * gg : B * gg + B].rearrange("p (th tl) c -> p th c tl", tl=2),
+                    out=g_t[:, B * gg : B * gg + B, :].rearrange("p (c i) t -> p c t i", i=4),
+                    in0=u_t[:, :, B * gg : B * gg + B].rearrange("p t (c i) -> p c t i", i=4),
                     scalar1=mx_b[:],
                     scalar2=nmn_b[:],
                     op0=ALU.subtract,

@@ -32,9 +32,9 @@ def tile_lagrangenet_kernel(tc, x, min_x, max_x, W_words, W_scales, dof, out):
     with ExitStack() as ctx:
         const = ctx.enter_context(tc.tile_pool(name="const", bufs=1))
         wpool = ctx.enter_context(tc.tile_pool(name="wpool", bufs=UNITS))
-        upool = ctx.enter_context(tc.tile_pool(name="upool", bufs=3))
-        gpool = ctx.enter_context(tc.tile_pool(name="gpool", bufs=3))
-        cpool = ctx.enter_context(tc.tile_pool(name="cpool", bufs=4))
+        upool = ctx.enter_context(tc.tile_pool(name="upool", bufs=2))
+        gpool = ctx.enter_context(tc.tile_pool(name="gpool", bufs=2))
+        cpool = ctx.enter_context(tc.tile_pool(name="cpool", bufs=3))
         opool = ctx.enter_context(tc.tile_pool(name="opool", bufs=4))
         accp = ctx.enter_context(tc.psum_pool(name="accp", bufs=1))
         bcp = ctx.enter_context(tc.psum_pool(name="bcp", bufs=4))
@@ -164,7 +164,7 @@ def tile_lagrangenet_kernel(tc, x, min_x, max_x, W_words, W_scales, dof, out):
                 spread_group(bc[:, B * gg : B * gg + B], g, xm[:, g // 16, :])
 
         def mx_pass(g, h, nh, codes, plane):
-            cols = slice(B * (g % 2) + P * h, B * (g % 2) + P * h + P)
+            cols = slice(B * (g % 4) + P * h, B * (g % 4) + P * h + P)
             nc.tensor.matmul_mx(
                 out=acc[h][nh][:],
                 lhsT=codes[:, cols].bitcast(FP8X4),
@@ -178,63 +178,61 @@ def tile_lagrangenet_kernel(tc, x, min_x, max_x, W_words, W_scales, dof, out):
         for k in range(4):
             spread(k)
 
-        for u in range(UNITS):
-            bc = bc_tiles[u // 2][:, 512 * (u % 2) : 512 * (u % 2) + 512]
-            u_t = upool.tile([P, 4, 512], F32)
-            for t in range(4):
-                nc.scalar.activation(
-                    out=u_t[:, t, :],
-                    in_=bc,
-                    func=ACTF.Abs,
-                    bias=nbias[:, t : t + 1],
-                    scale=float(DOF - 1),
-                )
-            g_t = gpool.tile([P, 512, 4], BF16, align_bytes=64)
-            codes = cpool.tile([P, 512], U32, align_bytes=64)
-            plane = cpool.tile([P, 512], U8, align_bytes=64)
+        for k in range(BANKS):
+            bc = bc_tiles[k]
+            u_t = upool.tile([P, 4, 4 * B], F32)
+            g_t = gpool.tile([P, 4 * B, 4], BF16, align_bytes=64)
+            codes = cpool.tile([P, 4 * B], U32, align_bytes=64)
+            plane = cpool.tile([P, 4 * B], U8, align_bytes=64)
 
-            def finish(gg):
+            def finish(lo):
                 nc.vector.tensor_scalar(
-                    out=g_t[:, B * gg : B * gg + B, :].rearrange("p (c i) t -> p c t i", i=4),
-                    in0=u_t[:, :, B * gg : B * gg + B].rearrange("p t (c i) -> p c t i", i=4),
+                    out=g_t[:, lo : lo + B, :].rearrange("p (c i) t -> p c t i", i=4),
+                    in0=u_t[:, :, lo : lo + B].rearrange("p t (c i) -> p c t i", i=4),
                     scalar1=mx_b[:],
                     scalar2=nmn_b[:],
                     op0=ALU.subtract,
                     op1=ALU.min,
                 )
 
-            def quantise(gg):
+            def quantise(lo):
                 nc.vector.quantize_mx(
-                    out=codes[:, B * gg : B * gg + B].bitcast(FP8X4),
-                    scales=plane[:, B * gg : B * gg + B],
-                    in_=g_t[:, B * gg : B * gg + B, :].rearrange("p c t -> p (c t)"),
+                    out=codes[:, lo : lo + B].bitcast(FP8X4),
+                    scales=plane[:, lo : lo + B],
+                    in_=g_t[:, lo : lo + B, :].rearrange("p c t -> p (c t)"),
                 )
 
-            if u == 0:
-                finish(0)
-                quantise(0)
-                finish(1)
-                quantise(1)
-            else:
-                finish(0)
-                finish(1)
-                quantise(0)
-                quantise(1)
+            chunks = [(0, 512), (512, 768), (768, 1024)] if k == BANKS - 1 else [(0, 1024)]
+            for lo, hi in chunks:
+                for t in range(4):
+                    nc.scalar.activation(
+                        out=u_t[:, t, lo:hi],
+                        in_=bc[:, lo:hi],
+                        func=ACTF.Abs,
+                        bias=nbias[:, t : t + 1],
+                        scale=float(DOF - 1),
+                    )
+                starts = list(range(lo, hi, B))
+                for i, a in enumerate(starts):
+                    finish(a)
+                    if i > 0:
+                        quantise(starts[i - 1])
+                quantise(starts[-1])
 
-            if u % 2 == 1 and u // 2 + 4 < BANKS:
-                spread(u // 2 + 4)
+                if hi == 4 * B and k + 4 < BANKS:
+                    spread(k + 4)
 
-            for gg in range(2):
-                g = 2 * u + gg
-                for h in range(2):
-                    for nh in range(2):
-                        mx_pass(g, h, nh, codes, plane)
-                        if g == GROUPS - 1:
-                            o_t = opool.tile([P, 512], F32)
-                            if nh == 0:
-                                nc.scalar.mul(out=o_t[:], in_=acc[h][nh][:], mul=-1.0)
-                            else:
-                                nc.vector.tensor_scalar_mul(out=o_t[:], in0=acc[h][nh][:], scalar1=-1.0)
-                            nc.sync.dma_start(
-                                out=out[P * h : P * h + P, 512 * nh : 512 * nh + 512], in_=o_t[:]
-                            )
+                for a in starts:
+                    g = 4 * k + a // B
+                    for h in range(2):
+                        for nh in range(2):
+                            mx_pass(g, h, nh, codes, plane)
+                            if g == GROUPS - 1:
+                                o_t = opool.tile([P, 512], F32)
+                                if nh == 0:
+                                    nc.scalar.mul(out=o_t[:], in_=acc[h][nh][:], mul=-1.0)
+                                else:
+                                    nc.vector.tensor_scalar_mul(out=o_t[:], in0=acc[h][nh][:], scalar1=-1.0)
+                                nc.sync.dma_start(
+                                    out=out[P * h : P * h + P, 512 * nh : 512 * nh + 512], in_=o_t[:]
+                                )

from contextlib import ExitStack

import concourse.masks as masks
import concourse.mybir as mybir

FP8X4 = mybir.dt.float8_e4m3fn_x4
BF16 = mybir.dt.bfloat16
F32 = mybir.dt.float32
I32 = mybir.dt.int32
U32 = mybir.dt.uint32
U8 = mybir.dt.uint8
ALU = mybir.AluOpType
ACTF = mybir.ActivationFunctionType

P = 128
B = 256
F = 256
DOF = 64
N = 1024
K = F * DOF
GROUPS = K // 512
SETS = 4
PER_SET = GROUPS // SETS
UNITS = GROUPS // 2
BANKS = GROUPS // 4
FLOPS = 2 * B * K * N


def tile_lagrangenet_kernel(tc, x, min_x, max_x, W_words, W_scales, dof, out):
    nc = tc.nc
    assert dof == DOF
    with ExitStack() as ctx:
        const = ctx.enter_context(tc.tile_pool(name="const", bufs=1))
        wpool = ctx.enter_context(tc.tile_pool(name="wpool", bufs=UNITS))
        upool = ctx.enter_context(tc.tile_pool(name="upool", bufs=2))
        gpool = ctx.enter_context(tc.tile_pool(name="gpool", bufs=2))
        cpool = ctx.enter_context(tc.tile_pool(name="cpool", bufs=3))
        opool = ctx.enter_context(tc.tile_pool(name="opool", bufs=4))
        accp = ctx.enter_context(tc.psum_pool(name="accp", bufs=1))
        bcp = ctx.enter_context(tc.psum_pool(name="bcp", bufs=4))
        ctx.enter_context(tc.manual_schedule())

        x_sb = const.tile([P, 2, F], BF16)
        nc.scalar.dma_start(out=x_sb[:], in_=x.rearrange("(h p) f -> p h f", p=P))
        mn_b = const.tile([P, 1], BF16)
        nc.scalar.dma_start(out=mn_b[:], in_=min_x.partition_broadcast(P))
        mx_b = const.tile([P, 1], BF16)
        nc.scalar.dma_start(out=mx_b[:], in_=max_x.partition_broadcast(P))

        warm = const.tile([P, 1], F32)
        nc.vector.memset(warm[:], 0.0)

        wsc = const.tile([P, PER_SET, N], U8, align_bytes=64)
        nc.vector.memset(wsc[:].rearrange("p c n -> p (c n)").bitcast(I32), 0)
        w_view = W_words.bitcast(I32).rearrange("g p n o -> p g (n o)")
        s_view = W_scales.bitcast(I32).rearrange("(c j) (q r) n -> q r j c n", j=SETS, r=4)

        w_tiles = []
        for u in range(UNITS):
            w_t = wpool.tile([P, 2, N], U32, align_bytes=64)
            w_tiles.append(w_t)
            if u == 0 or u == UNITS - 1:
                nc.sync.dma_start(out=w_t[:, 0:1, :].bitcast(I32), in_=w_view[:, 2 * u : 2 * u + 1, :])
                if u == 0:
                    for q in range(4):
                        for r in range(4):
                            nc.sync.dma_start(
                                out=wsc[32 * q + r : 32 * q + 16 : 4, :, :].bitcast(I32), in_=s_view[q, r]
                            )
                nc.sync.dma_start(out=w_t[:, 1:2, :].bitcast(I32), in_=w_view[:, 2 * u + 1 : 2 * u + 2, :])
            else:
                nc.sync.dma_start(out=w_t[:].bitcast(I32), in_=w_view[:, 2 * u : 2 * u + 2, :])

        warm2 = const.tile([P, 1], F32)
        nc.scalar.activation(out=warm2[:], in_=warm[:], func=ACTF.Abs)

        ident = const.tile([P, P], BF16)
        masks.make_identity(nc, ident[:])
        p_int = const.tile([P, 4], I32)
        nc.gpsimd.iota(p_int[:], pattern=[[1, 4]], base=0, channel_multiplier=4)

        rep = const.tile([P, 16 * P], BF16)

        def rep_views(b4):
            return (
                rep[:, 512 * b4 : 512 * b4 + 512].rearrange("p (f r) -> p f r", r=16),
                ident[:, 32 * b4 : 32 * b4 + 32].unsqueeze(2).to_broadcast([P, 32, 16]),
            )

        dst, src = rep_views(0)
        nc.vector.tensor_copy(out=dst, in_=src)
        dst, src = rep_views(1)
        nc.scalar.copy(out=dst, in_=src)
        for b4 in range(2, 4):
            dst, src = rep_views(b4)
            nc.gpsimd.tensor_scalar(out=dst, in0=src, scalar1=1.0, scalar2=0.0, op0=ALU.mult, op1=ALU.add)

        p_and = const.tile([P, 4], I32)
        nc.vector.tensor_single_scalar(out=p_and[:], in_=p_int[:], scalar=DOF - 1, op=ALU.bitwise_and)
        p_f = const.tile([P, 4], F32)
        nc.vector.tensor_copy(out=p_f[:], in_=p_and[:])

        cst = const.tile([P, 4], F32)
        rng = cst[:, 0:1]
        nrng = cst[:, 1:2]
        c63 = cst[:, 2:3]
        nc.vector.tensor_sub(out=nrng, in0=mn_b[:], in1=mx_b[:])
        nc.vector.tensor_scalar_mul(out=c63, in0=mn_b[:], scalar1=-float(DOF - 1))
        nbias = const.tile([P, 4], F32)
        nc.vector.tensor_scalar(
            out=nbias[:], in0=p_f[:], scalar1=nrng, scalar2=c63, op0=ALU.mult, op1=ALU.add
        )
        nc.vector.tensor_sub(out=rng, in0=mx_b[:], in1=mn_b[:])
        nmn_b = const.tile([P, 1], BF16)

        xt_ps = bcp.tile([P, 2, B], BF16, tag="bc")
        for hf in range(2):
            for h in range(2):
                nc.tensor.transpose(
                    xt_ps[:, hf, P * h : P * h + P], x_sb[:, h, P * hf : P * hf + P], ident[:]
                )

        def spread_group(dst_ps, g, rhs):
            nc.tensor.matmul(
                dst_ps, lhsT=rep[:, P * (g % 16) : P * (g % 16) + P], rhs=rhs, start=True, stop=True
            )

        xm = const.tile([P, 2, B], BF16)
        below = const.tile([P, 2, B], F32)
        side = const.tile([P, 2, B], F32)
        for hf in range(2):
            nc.vector.tensor_scalar(
                out=below[:, hf, :], in0=xt_ps[:, hf, :], scalar1=mn_b[:], scalar2=None, op0=ALU.is_lt
            )
            nc.vector.scalar_tensor_tensor(
                out=side[:, hf, :],
                in0=xt_ps[:, hf, :],
                scalar=mx_b[:],
                in1=below[:, hf, :],
                op0=ALU.is_gt,
                op1=ALU.subtract,
            )
            nc.vector.scalar_tensor_tensor(
                out=xm[:, hf, :],
                in0=side[:, hf, :],
                scalar=rng,
                in1=xt_ps[:, hf, :],
                op0=ALU.mult,
                op1=ALU.add,
            )
        nc.vector.tensor_scalar_mul(out=nmn_b[:], in0=mn_b[:], scalar1=-1.0)

        acc = [
            [accp.tile([P, 512], F32, name="acc%d%d" % (h, nh)) for nh in range(2)] for h in range(2)
        ]

        bc_tiles = {}

        def spread(k):
            bc = bcp.tile([P, 4 * B], BF16, tag="bc")
            bc_tiles[k] = bc
            for gg in range(4):
                g = 4 * k + gg
                spread_group(bc[:, B * gg : B * gg + B], g, xm[:, g // 16, :])

        def mx_pass(g, h, nh, codes, plane):
            cols = slice(B * (g % 4) + P * h, B * (g % 4) + P * h + P)
            nc.tensor.matmul_mx(
                out=acc[h][nh][:],
                lhsT=codes[:, cols].bitcast(FP8X4),
                lhsT_scale=plane[:, cols],
                rhs=w_tiles[g // 2][:, g % 2, 512 * nh : 512 * nh + 512].bitcast(FP8X4),
                rhs_scale=wsc[4 * (g % 4) : P, g // 4, 512 * nh : 512 * nh + 512],
                start=(g == 0),
                stop=(g == GROUPS - 1),
            )

        for k in range(4):
            spread(k)

        for k in range(BANKS):
            bc = bc_tiles[k]
            u_t = upool.tile([P, 4, 4 * B], F32)
            g_t = gpool.tile([P, 4 * B, 4], BF16, align_bytes=64)
            codes = cpool.tile([P, 4 * B], U32, align_bytes=64)
            plane = cpool.tile([P, 4 * B], U8, align_bytes=64)

            def finish(lo):
                nc.vector.tensor_scalar(
                    out=g_t[:, lo : lo + B, :].rearrange("p (c i) t -> p c t i", i=4),
                    in0=u_t[:, :, lo : lo + B].rearrange("p t (c i) -> p c t i", i=4),
                    scalar1=mx_b[:],
                    scalar2=nmn_b[:],
                    op0=ALU.subtract,
                    op1=ALU.min,
                )

            def quantise(lo):
                nc.vector.quantize_mx(
                    out=codes[:, lo : lo + B].bitcast(FP8X4),
                    scales=plane[:, lo : lo + B],
                    in_=g_t[:, lo : lo + B, :].rearrange("p c t -> p (c t)"),
                )

            chunks = [(0, 512), (512, 768), (768, 1024)] if k == BANKS - 1 else [(0, 1024)]
            for lo, hi in chunks:
                for t in range(4):
                    nc.scalar.activation(
                        out=u_t[:, t, lo:hi],
                        in_=bc[:, lo:hi],
                        func=ACTF.Abs,
                        bias=nbias[:, t : t + 1],
                        scale=float(DOF - 1),
                    )
                starts = list(range(lo, hi, B))
                for i, a in enumerate(starts):
                    finish(a)
                    if i > 0:
                        quantise(starts[i - 1])
                quantise(starts[-1])

                if hi == 4 * B and k + 4 < BANKS:
                    spread(k + 4)

                for a in starts:
                    g = 4 * k + a // B
                    for h in range(2):
                        for nh in range(2):
                            mx_pass(g, h, nh, codes, plane)
                            if g == GROUPS - 1:
                                o_t = opool.tile([P, 512], F32)
                                if nh == 0:
                                    nc.scalar.mul(out=o_t[:], in_=acc[h][nh][:], mul=-1.0)
                                else:
                                    nc.vector.tensor_scalar_mul(out=o_t[:], in0=acc[h][nh][:], scalar1=-1.0)
                                nc.sync.dma_start(
                                    out=out[P * h : P * h + P, 512 * nh : 512 * nh + 512], in_=o_t[:]
                                )
